import numpy as np
import ml_dtypes


def mxq(x, axis, fmt="e4m3"):
    dtype, down = {"e4m3": (ml_dtypes.float8_e4m3fn, 7), "e5m2": (ml_dtypes.float8_e5m2, 14)}[fmt]
    v = np.moveaxis(np.asarray(x, np.float32).astype(ml_dtypes.bfloat16).astype(np.float64), axis, -1)
    blocks = v.reshape(v.shape[:-1] + (-1, 32))
    amax = np.abs(blocks).max(-1, keepdims=True)
    byte = np.maximum(np.where(amax > 0, np.frexp(amax)[1] - 1 + 127, 0) - down, 1)
    scale = np.exp2(byte - 127.0)
    codes = (blocks / scale).astype(np.float32).astype(dtype).astype(np.float64)
    return np.moveaxis((codes * scale).reshape(v.shape), -1, axis)


WIDE = False


def mx_kscale(k):
    if not WIDE:
        return np.ones(k)
    levels = np.array([10, -10, 5, -5, 0])
    if k % 512:
        return np.exp2(np.random.permutation(np.resize(levels, k // 32))).repeat(32)
    a = np.empty((k // 512, 16))
    for p in range(k // 512):
        a[p, :8] = np.random.permutation(np.resize(levels, 8))
        for g in range(8):
            far = levels[np.abs(levels - a[p, g]) >= 10]
            a[p, g + 8] = far[np.random.randint(len(far))]
    return np.exp2(a.ravel()).repeat(32)


BF16 = ml_dtypes.bfloat16


def bf(x):
    return np.asarray(x, np.float32).astype(BF16)


def f64(x):
    return np.asarray(x).astype(np.float64)


Nc, Ns, Nt, d_h, BS = 64, 64, 16, 128, 16
I, J = Ns * Nt, Nc * Nt
T = BS * d_h


def setup_inputs():
    s = mx_kscale(T).reshape(BS, d_h)[:, None, None, :]
    u = mx_kscale(I)
    Ac = (np.random.random((Ns, Nc)) < 3.2 / Ns).astype(np.float64)
    Ac[np.random.randint(0, Ns, Nc), np.arange(Nc)] = 1.0
    Ac[np.arange(Ns), np.random.randint(0, Nc, Ns)] = 1.0
    As = (np.random.random((Ns, Ns)) < 0.05).astype(np.float64)
    AA = np.dot(np.dot(As, As), Ac) + np.dot(As, Ac) + Ac
    AA = (AA != 0).astype(np.float64)
    AA_mask = bf(np.tile(AA, (Nt, Nt)))
    g = 1.0 / np.sqrt(0.5 * J * AA.mean())
    w = np.random.standard_normal((I, J)) * g
    w = np.where(np.abs(w) < 1e-3, np.copysign(1e-3, w), w)
    GCW0 = bf(w)
    GCB = bf(np.random.standard_normal((I, d_h)) * 0.5)
    h0 = bf(np.random.standard_normal((BS, Nc, Nt, d_h)))
    e = bf(np.random.standard_normal(1) * 0.1)
    go = np.random.standard_normal((BS, Ns, Nt, d_h)) * np.exp2(np.random.randint(-6, 1, (BS, Ns, Nt, 1))) * 2.0
    A0 = np.maximum(f64(AA_mask) * f64(GCW0), 0.0)
    x0 = np.transpose(f64(h0), (0, 2, 1, 3)).reshape(BS, J, d_h)
    z = A0 @ x0 + f64(GCB)
    zo = np.transpose(z.reshape(BS, Nt, Ns, d_h), (0, 2, 1, 3))
    go = go * (np.abs(zo) > 1e-4)
    go = go * u.reshape(Nt, Ns).T[None, :, :, None] / s
    return {"h": bf(f64(h0) * s), "e": e, "AA_mask": AA_mask, "GCW": bf(f64(GCW0) / u[:, None]), "GCB": GCB,
            "z": np.asarray(z, np.float32), "grad_out": bf(go)}


def reference(h, e, AA_mask, GCW, GCB, z, grad_out):
    bs = grad_out.shape[0]
    mw = f64(AA_mask) * f64(GCW)
    A = np.maximum(mw, 0.0)
    g = np.transpose(f64(grad_out), (0, 2, 1, 3)).reshape(bs, I, d_h)
    dz = g * (f64(z) > 0.0)
    dzm = np.transpose(dz, (1, 0, 2)).reshape(I, bs * d_h)
    xm = np.transpose(f64(h), (2, 1, 0, 3)).reshape(J, bs * d_h)
    gx = mxq(A, 0, "e4m3").T @ mxq(dzm, 0, "e5m2")
    dA = mxq(dzm, 1, "e5m2") @ mxq(xm, 1, "e4m3").T
    dh = np.transpose(gx.reshape(Nt, Nc, bs, d_h), (2, 1, 0, 3))
    dW = dA * (mw > 0.0)
    return dh, dW

@@ -1,0 +1,219 @@
+from contextlib import ExitStack
+
+import concourse.mybir as mybir
+from concourse.masks import make_identity
+
+FLOPS = 2 * 2 * 1024 * 1024 * 2048
+BYTES = (4 + 2 + 2 + 8 + 4 + 8 + 4) * 1024 * 1024
+
+F32 = mybir.dt.float32
+BF16 = mybir.dt.bfloat16
+U32 = mybir.dt.uint32
+U8 = mybir.dt.uint8
+E4 = mybir.dt.float8_e4m3fn_x4
+E5 = mybir.dt.float8_e5m2_x4
+ALU = mybir.AluOpType
+
+P = 128
+
+
+def tile_gcnfast_t_v_kernel(tc, h, e, AA_mask, GCW, GCB, z, grad_out, out_0, out_1):
+    nc = tc.nc
+
+    z_v = z.rearrange("b (t g r j) d -> b g t r (j d)", t=16, g=2, r=8, j=4)
+    go_v = grad_out.rearrange("b (g r j) t d -> b g t (r j) d", g=2, r=8, j=4)
+    w_v = GCW.rearrange("(t g r j) w -> g t r (j w)", t=16, g=2, r=8, j=4)
+    m_v = AA_mask.rearrange("(t g r j) w -> g t r (j w)", t=16, g=2, r=8, j=4)
+    o1_v = out_1.rearrange("(t g r j) w -> g j t r w", t=16, g=2, r=8, j=4)
+    h_v = h.rearrange("b c (ph r) d -> (c ph) b (r d)", ph=2, r=8)
+    o0_v = out_0.rearrange("b c (ph rh r) d -> rh (c ph) b (r d)", ph=2, rh=2, r=4)
+
+    with ExitStack() as ctx:
+        keep = ctx.enter_context(tc.tile_pool(name="keep", bufs=1))
+        stream = ctx.enter_context(tc.tile_pool(name="stream", bufs=2))
+        shared = ctx.enter_context(tc.tile_pool(name="shared", bufs=8))
+        tpool = ctx.enter_context(tc.psum_pool(name="tpool", bufs=4))
+        apool = ctx.enter_context(tc.psum_pool(name="apool", bufs=4))
+
+        ident = keep.tile([P, P], F32)
+        make_identity(nc, ident[:])
+
+        mw = keep.tile([P, 2, 4096], BF16)
+        a_c = keep.tile([P, 2, 1024], U32, align_bytes=64)
+        a_s = keep.tile([P, 2, 1024], U8, align_bytes=64)
+        xt_c = keep.tile([P, 4, 1024], U32, align_bytes=64)
+        xt_s = keep.tile([P, 4, 1024], U8, align_bytes=64)
+        da_c = keep.tile([P, 4, 2, 512], U32, align_bytes=64)
+        da_s = keep.tile([P, 4, 2, 512], U8, align_bytes=64)
+        dt_c = keep.tile([P, 4, 1024], U32, align_bytes=64)
+        dt_s = keep.tile([P, 4, 1024], U8, align_bytes=64)
+
+        def load_unit(q, g):
+            zu = stream.tile([P, 4, 512], F32, tag="zu", bufs=3)
+            gu = stream.tile([P, 4, 512], BF16, tag="gu", bufs=3)
+            for bl in range(4):
+                b = 4 * q + bl
+                nc.sync.dma_start(out=zu[:, bl, :], in_=z_v[b, g])
+                nc.sync.dma_start(out=gu[:, bl, :].rearrange("p (j d) -> p j d", j=4), in_=go_v[b, g])
+            return zu, gu
+
+        def load_h(q):
+            hq = shared.tile([P, 4, 1024], BF16, tag="s8", align_bytes=64)
+            nc.sync.dma_start(out=hq[:], in_=h_v[:, 4 * q : 4 * q + 4, :])
+            return hq
+
+        def load_a(g):
+            wr = shared.tile([P, 4096], BF16, tag="s8", align_bytes=64)
+            mr = shared.tile([P, 4096], BF16, tag="s8", align_bytes=64)
+            nc.sync.dma_start(out=wr[:], in_=w_v[g])
+            nc.sync.dma_start(out=mr[:], in_=m_v[g])
+            return wr, mr
+
+        def unit(q, g, zu, gu):
+            du = stream.tile([P, 4, 512], BF16, tag="du", bufs=2, align_bytes=64)
+            for bl in range(4):
+                nc.vector.scalar_tensor_tensor(
+                    out=du[:, :, 128 * bl : 128 * (bl + 1)],
+                    in0=zu[:, bl, :].rearrange("p (j d) -> p j d", j=4),
+                    scalar=0.0,
+                    in1=gu[:, bl, :].rearrange("p (j d) -> p j d", j=4),
+                    op0=ALU.is_gt,
+                    op1=ALU.mult,
+                )
+            dw = du[:].rearrange("p j c -> p (j c)").bitcast(F32)
+            dti = stream.tile([P, 2048], BF16, tag="dti", bufs=2, align_bytes=64)
+            dtw = dti[:].bitcast(F32).rearrange("k (a j p u) -> k a j p u", a=2, j=2, p=128, u=2)
+            for a in range(2):
+                tp = tpool.tile([P, 2, 2, 128], F32, tag="tp")
+                for j in range(2):
+                    jj = 2 * a + j
+                    for u in range(2):
+                        nc.tensor.transpose(tp[:, j, u, :], dw[:, 256 * jj + u : 256 * (jj + 1) : 2], ident[:])
+                nc.scalar.copy(out=dtw[:, a], in_=tp[:].rearrange("k j u p -> k j p u"))
+            di = stream.tile([P, 512, 4], BF16, tag="di", bufs=2, align_bytes=64)
+            nc.vector.tensor_copy(out=di[:], in_=du[:].rearrange("p j c -> p c j"))
+            nc.vector.quantize_mx(
+                out=da_c[:, q, g, :].bitcast(E5),
+                scales=da_s[:, q, g, :],
+                in_=di[:].rearrange("p c j -> p (c j)"),
+            )
+            nc.vector.quantize_mx(
+                out=dt_c[:, q, 512 * g : 512 * (g + 1)].bitcast(E5),
+                scales=dt_s[:, q, 512 * g : 512 * (g + 1)],
+                in_=dti[:],
+            )
+
+        def xpath(q, hq):
+            hw = hq[:].rearrange("p b x -> p (b x)").bitcast(F32)
+            hw = hw.rearrange("p (b r k u) -> p u r b k", b=4, r=8, k=32, u=2)
+            x2 = shared.tile([P, 8, 2, 128], F32, tag="s8", align_bytes=64)
+            for u in range(2):
+                nc.scalar.copy(out=x2[:, :, u, :].rearrange("p r (b k) -> p r b k", b=4), in_=hw[:, u])
+            xti = shared.tile([P, 4096], BF16, tag="s8", align_bytes=64)
+            xtw = xti[:].bitcast(F32).rearrange("k (ph a r c u) -> k a ph r c u", ph=2, a=4, r=2, c=64, u=2)
+            for a in range(4):
+                tp = tpool.tile([P, 2, 2, 128], F32, tag="tp")
+                for r in range(2):
+                    for u in range(2):
+                        nc.tensor.transpose(tp[:, r, u, :], x2[:, 2 * a + r, u, :], ident[:])
+                nc.scalar.copy(out=xtw[:, a], in_=tp[:].rearrange("k r u (c ph) -> k ph r c u", ph=2))
+            nc.vector.quantize_mx(out=xt_c[:, q, :].bitcast(E4), scales=xt_s[:, q, :], in_=xti[:])
+
+        def a_prep(g, wr, mr):
+            nc.vector.tensor_tensor(out=mw[:, g, :], in0=wr[:], in1=mr[:], op=ALU.mult)
+            ai = shared.tile([P, 512, 2, 4], BF16, tag="s8", align_bytes=64)
+            nc.vector.tensor_scalar(
+                out=ai[:],
+                in0=mw[:, g, :].rearrange("p (j ph x) -> p x ph j", j=4, ph=2),
+                scalar1=0.0,
+                scalar2=None,
+                op0=ALU.max,
+            )
+            nc.vector.quantize_mx(
+                out=a_c[:, g, :].bitcast(E4),
+                scales=a_s[:, g, :],
+                in_=ai[:].rearrange("p x ph j -> p (x ph j)"),
+            )
+
+        def gx(q):
+            for rh in range(2):
+                oh = shared.tile([P, 4, 4, 128], F32, tag="s8", align_bytes=64)
+                for r in range(4):
+                    cols = slice(128 * (4 * rh + r), 128 * (4 * rh + r + 1))
+                    acc = apool.tile([P, 512], F32, tag="acc")
+                    for g in range(2):
+                        nc.tensor.matmul_mx(
+                            out=acc[:],
+                            lhsT=a_c[:, g, cols].bitcast(E4),
+                            lhsT_scale=a_s[:, g, cols],
+                            rhs=da_c[:, q, g, :].bitcast(E5),
+                            rhs_scale=da_s[:, q, g, :],
+                            start=(g == 0),
+                            stop=(g == 1),
+                        )
+                    nc.scalar.copy(out=oh[:, :, r, :], in_=acc[:].rearrange("p (b d) -> p b d", b=4))
+                nc.scalar.dma_start(
+                    out=o0_v[rh][:, 4 * q : 4 * q + 4, :], in_=oh[:].rearrange("p b r d -> p b (r d)")
+                )
+
+        def da(g):
+            for jj in range(4):
+                wo = stream.tile([P, 1024], F32, tag="wo", bufs=3)
+                cols = slice(512 * g + 128 * jj, 512 * g + 128 * (jj + 1))
+                for nh in range(2):
+                    ncols = slice(512 * nh, 512 * (nh + 1))
+                    acc = apool.tile([P, 512], F32, tag="acc")
+                    for q in range(4):
+                        nc.tensor.matmul_mx(
+                            out=acc[:],
+                            lhsT=dt_c[:, q, cols].bitcast(E5),
+                            lhsT_scale=dt_s[:, q, cols],
+                            rhs=xt_c[:, q, ncols].bitcast(E4),
+                            rhs_scale=xt_s[:, q, ncols],
+                            start=(q == 0),
+                            stop=(q == 3),
+                        )
+                    nc.vector.scalar_tensor_tensor(
+                        out=wo[:, ncols],
+                        in0=mw[:, g, 1024 * jj + 512 * nh : 1024 * jj + 512 * (nh + 1)],
+                        scalar=0.0,
+                        in1=acc[:],
+                        op0=ALU.is_gt,
+                        op1=ALU.mult,
+                    )
+                nc.sync.dma_start(out=o1_v[g, jj], in_=wo[:])
+
+        u00 = load_unit(0, 0)
+        h0 = load_h(0)
+        u10 = load_unit(1, 0)
+        h1 = load_h(1)
+        unit(0, 0, u00[0], u00[1])
+        xpath(0, h0)
+        u20 = load_unit(2, 0)
+        h2 = load_h(2)
+        unit(1, 0, u10[0], u10[1])
+        xpath(1, h1)
+        u30 = load_unit(3, 0)
+        h3 = load_h(3)
+        unit(2, 0, u20[0], u20[1])
+        xpath(2, h2)
+        a0 = load_a(0)
+        a1 = load_a(1)
+        u01 = load_unit(0, 1)
+        unit(3, 0, u30[0], u30[1])
+        xpath(3, h3)
+        u11 = load_unit(1, 1)
+        a_prep(0, a0[0], a0[1])
+        a_prep(1, a1[0], a1[1])
+        da(0)
+        unit(0, 1, u01[0], u01[1])
+        u21 = load_unit(2, 1)
+        gx(0)
+        unit(1, 1, u11[0], u11[1])
+        u31 = load_unit(3, 1)
+        gx(1)
+        unit(2, 1, u21[0], u21[1])
+        gx(2)
+        unit(3, 1, u31[0], u31[1])
+        gx(3)
+        da(1)

@@ -13,8 +13,49 @@ U8 = mybir.dt.uint8
 E4 = mybir.dt.float8_e4m3fn_x4
 E5 = mybir.dt.float8_e5m2_x4
 ALU = mybir.AluOpType
+ACTF = mybir.ActivationFunctionType
 
 P = 128
+
+ORDER = [
+    ("LU", 0), ("LH", 0), ("stt", 0), ("LA", 1), ("LA", 0), ("T", 0, 0),
+    ("ilv", 0), ("tt", 1), ("qa", 0), ("ed", 0, 0), ("T", 0, 1), ("LU", 1),
+    ("LH", 1), ("tt", 0), ("stt", 1), ("LH", 2), ("x2", 0), ("xT", 0, 0),
+    ("ilv", 1), ("ed", 0, 1), ("xT", 0, 1), ("ex", 0, 0), ("LU", 2), ("ex", 0, 1),
+    ("aiV", 0), ("xT", 0, 2), ("LU", 3), ("ex", 0, 2), ("xT", 0, 3), ("ex", 0, 3),
+    ("aiS", 1), ("T", 1, 0), ("qx", 0), ("ed", 1, 0), ("x2", 1), ("x2", 2),
+    ("xT", 1, 0), ("stt", 2), ("T", 1, 1), ("qb", 0), ("ex", 1, 0), ("qa", 1),
+    ("xT", 1, 1), ("ed", 1, 1), ("qA", 0), ("xT", 2, 0), ("ex", 1, 1), ("ex", 2, 0),
+    ("xT", 1, 2), ("xT", 1, 3), ("ex", 1, 2), ("stt", 3), ("ilv", 2), ("qb", 1),
+    ("qA", 1), ("T", 2, 0), ("ex", 1, 3), ("qa", 2), ("LH", 3), ("T", 2, 1),
+    ("ed", 2, 0), ("ed", 2, 1), ("LU", 4), ("qb", 2), ("xT", 2, 1), ("stt", 4),
+    ("xT", 2, 2), ("x2", 3), ("ex", 2, 1), ("ex", 2, 2), ("xT", 2, 3), ("xT", 3, 0),
+    ("ex", 2, 3), ("ilv", 4), ("LU", 7), ("ex", 3, 0), ("T", 3, 1), ("qa", 4),
+    ("T", 3, 0), ("qx", 1), ("ed", 3, 0), ("gx", 0, 0), ("ilv", 3), ("qx", 2),
+    ("gx", 0, 1), ("ed", 3, 1), ("xT", 3, 1), ("eo", 0, 0), ("eo", 0, 1), ("gx", 0, 2),
+    ("LU", 5), ("LU", 6), ("ex", 3, 1), ("eo", 0, 2), ("xT", 3, 2), ("xT", 3, 3),
+    ("ex", 3, 2), ("gx", 0, 3), ("gx", 0, 4), ("qb", 3), ("ex", 3, 3), ("eo", 0, 3),
+    ("qx", 3), ("da", 0, 0), ("T", 4, 0), ("ed", 4, 0), ("stt", 5), ("ilv", 5),
+    ("gx", 0, 5), ("da", 0, 1), ("qa", 5), ("eo", 0, 4), ("T", 4, 1), ("gx", 0, 6),
+    ("qa", 3), ("eo", 0, 5), ("ed", 4, 1), ("T", 5, 0), ("gx", 1, 0), ("eo", 0, 6),
+    ("stt", 6), ("ed", 5, 0), ("gx", 1, 1), ("da", 0, 2), ("eo", 1, 0), ("e1", 0, 0),
+    ("eo", 1, 1), ("gx", 1, 2), ("gx", 1, 3), ("eo", 1, 2), ("eo", 1, 3), ("e1", 0, 1),
+    ("da", 0, 3), ("gx", 0, 7), ("T", 6, 0), ("eo", 0, 7), ("gx", 1, 4), ("ilv", 6),
+    ("e1", 0, 2), ("qa", 6), ("T", 5, 1), ("eo", 1, 4), ("gx", 1, 5), ("qb", 4),
+    ("gx", 1, 6), ("stt", 7), ("ed", 5, 1), ("eo", 1, 5), ("da", 0, 4), ("e1", 0, 3),
+    ("gx", 1, 7), ("eo", 1, 6), ("ed", 6, 0), ("ilv", 7), ("da", 0, 5), ("eo", 1, 7),
+    ("qa", 7), ("T", 6, 1), ("e1", 0, 4), ("gx", 2, 0), ("e1", 0, 5), ("T", 7, 0),
+    ("eo", 2, 0), ("gx", 2, 1), ("gx", 2, 2), ("eo", 2, 1), ("da", 0, 6), ("eo", 2, 2),
+    ("gx", 3, 0), ("ed", 6, 1), ("eo", 3, 0), ("gx", 2, 3), ("da", 0, 7), ("eo", 2, 3),
+    ("gx", 2, 4), ("qb", 5), ("qb", 6), ("ed", 7, 0), ("gx", 2, 5), ("e1", 0, 6),
+    ("eo", 2, 4), ("gx", 2, 6), ("eo", 2, 5), ("gx", 2, 7), ("eo", 2, 6), ("T", 7, 1),
+    ("eo", 2, 7), ("ed", 7, 1), ("qb", 7), ("gx", 3, 1), ("gx", 3, 2), ("da", 1, 2),
+    ("eo", 3, 1), ("eo", 3, 2), ("gx", 3, 3), ("da", 1, 1), ("eo", 3, 3), ("gx", 3, 4),
+    ("e1", 0, 7), ("da", 1, 0), ("e1", 1, 0), ("gx", 3, 5), ("da", 1, 3), ("eo", 3, 4),
+    ("e1", 1, 1), ("gx", 3, 7), ("eo", 3, 5), ("e1", 1, 2), ("gx", 3, 6), ("da", 1, 6),
+    ("eo", 3, 6), ("da", 1, 4), ("e1", 1, 3), ("da", 1, 7), ("e1", 1, 6), ("da", 1, 5),
+    ("e1", 1, 7), ("e1", 1, 4), ("eo", 3, 7), ("e1", 1, 5),
+]
 
 
 def tile_gcnfast_t_v_kernel(tc, h, e, AA_mask, GCW, GCB, z, grad_out, out_0, out_1):
@@ -32,8 +73,7 @@ def tile_gcnfast_t_v_kernel(tc, h, e, AA_mask, GCW, GCB, z, grad_out, out_0, out
         keep = ctx.enter_context(tc.tile_pool(name="keep", bufs=1))
         stream = ctx.enter_context(tc.tile_pool(name="stream", bufs=2))
         shared = ctx.enter_context(tc.tile_pool(name="shared", bufs=8))
-        tpool = ctx.enter_context(tc.psum_pool(name="tpool", bufs=4))
-        apool = ctx.enter_context(tc.psum_pool(name="apool", bufs=4))
+        psum = ctx.enter_context(tc.psum_pool(name="psum", bufs=2))
 
         ident = keep.tile([P, P], F32)
         make_identity(nc, ident[:])
@@ -48,28 +88,32 @@ def tile_gcnfast_t_v_kernel(tc, h, e, AA_mask, GCW, GCB, z, grad_out, out_0, out
         dt_c = keep.tile([P, 4, 1024], U32, align_bytes=64)
         dt_s = keep.tile([P, 4, 1024], U8, align_bytes=64)
 
-        def load_unit(q, g):
-            zu = stream.tile([P, 4, 512], F32, tag="zu", bufs=3)
-            gu = stream.tile([P, 4, 512], BF16, tag="gu", bufs=3)
+        live = {}
+
+        def op_lu(n):
+            q, g = n % 4, n // 4
+            zu = stream.tile([P, 4, 512], F32, tag="zu", bufs=4)
+            gu = stream.tile([P, 4, 512], BF16, tag="gu", bufs=4)
             for bl in range(4):
                 b = 4 * q + bl
                 nc.sync.dma_start(out=zu[:, bl, :], in_=z_v[b, g])
                 nc.sync.dma_start(out=gu[:, bl, :].rearrange("p (j d) -> p j d", j=4), in_=go_v[b, g])
-            return zu, gu
+            live[("u", n)] = (zu, gu)
 
-        def load_h(q):
+        def op_lh(q):
             hq = shared.tile([P, 4, 1024], BF16, tag="s8", align_bytes=64)
             nc.sync.dma_start(out=hq[:], in_=h_v[:, 4 * q : 4 * q + 4, :])
-            return hq
+            live[("h", q)] = hq
 
-        def load_a(g):
+        def op_la(g):
             wr = shared.tile([P, 4096], BF16, tag="s8", align_bytes=64)
             mr = shared.tile([P, 4096], BF16, tag="s8", align_bytes=64)
             nc.sync.dma_start(out=wr[:], in_=w_v[g])
             nc.sync.dma_start(out=mr[:], in_=m_v[g])
-            return wr, mr
+            live[("a", g)] = (wr, mr)
 
-        def unit(q, g, zu, gu):
+        def op_stt(n):
+            zu, gu = live[("u", n)]
             du = stream.tile([P, 4, 512], BF16, tag="du", bufs=2, align_bytes=64)
             for bl in range(4):
                 nc.vector.scalar_tensor_tensor(
@@ -80,47 +124,92 @@ def tile_gcnfast_t_v_kernel(tc, h, e, AA_mask, GCW, GCB, z, grad_out, out_0, out
                     op0=ALU.is_gt,
                     op1=ALU.mult,
                 )
+            live[("d", n)] = du
+
+        def op_t(n, a):
+            du = live[("d", n)]
             dw = du[:].rearrange("p j c -> p (j c)").bitcast(F32)
-            dti = stream.tile([P, 2048], BF16, tag="dti", bufs=2, align_bytes=64)
+            tp = psum.tile([P, 2, 2, 128], F32, tag="tp", bufs=2)
+            for j in range(2):
+                jj = 2 * a + j
+                for u in range(2):
+                    nc.tensor.transpose(tp[:, j, u, :], dw[:, 256 * jj + u : 256 * (jj + 1) : 2], ident[:])
+            live[("tp", n, a)] = tp
+
+        def op_ed(n, a):
+            if a == 0:
+                dti_new = stream.tile([P, 2048], BF16, tag="dti", bufs=2, align_bytes=64)
+                live[("dti", n)] = dti_new
+            dti = live[("dti", n)]
             dtw = dti[:].bitcast(F32).rearrange("k (a j p u) -> k a j p u", a=2, j=2, p=128, u=2)
-            for a in range(2):
-                tp = tpool.tile([P, 2, 2, 128], F32, tag="tp")
-                for j in range(2):
-                    jj = 2 * a + j
-                    for u in range(2):
-                        nc.tensor.transpose(tp[:, j, u, :], dw[:, 256 * jj + u : 256 * (jj + 1) : 2], ident[:])
-                nc.scalar.copy(out=dtw[:, a], in_=tp[:].rearrange("k j u p -> k j p u"))
+            tp = live[("tp", n, a)]
+            nc.scalar.copy(out=dtw[:, a], in_=tp[:].rearrange("k j u p -> k j p u"))
+
+        def op_ilv(n):
+            du = live[("d", n)]
             di = stream.tile([P, 512, 4], BF16, tag="di", bufs=2, align_bytes=64)
             nc.vector.tensor_copy(out=di[:], in_=du[:].rearrange("p j c -> p c j"))
+            live[("di", n)] = di
+
+        def op_ilvs(n):
+            du = live[("d", n)]
+            di = stream.tile([P, 512, 4], BF16, tag="di", bufs=2, align_bytes=64)
+            nc.scalar.copy(out=di[:], in_=du[:].rearrange("p j c -> p c j"))
+            live[("di", n)] = di
+
+        def op_qa(n):
+            q, g = n % 4, n // 4
+            di = live[("di", n)]
             nc.vector.quantize_mx(
                 out=da_c[:, q, g, :].bitcast(E5),
                 scales=da_s[:, q, g, :],
                 in_=di[:].rearrange("p c j -> p (c j)"),
             )
+
+        def op_qb(n):
+            q, g = n % 4, n // 4
+            dti = live[("dti", n)]
             nc.vector.quantize_mx(
                 out=dt_c[:, q, 512 * g : 512 * (g + 1)].bitcast(E5),
                 scales=dt_s[:, q, 512 * g : 512 * (g + 1)],
                 in_=dti[:],
             )
 
-        def xpath(q, hq):
+        def op_x2(q):
+            hq = live[("h", q)]
             hw = hq[:].rearrange("p b x -> p (b x)").bitcast(F32)
             hw = hw.rearrange("p (b r k u) -> p u r b k", b=4, r=8, k=32, u=2)
             x2 = shared.tile([P, 8, 2, 128], F32, tag="s8", align_bytes=64)
             for u in range(2):
                 nc.scalar.copy(out=x2[:, :, u, :].rearrange("p r (b k) -> p r b k", b=4), in_=hw[:, u])
-            xti = shared.tile([P, 4096], BF16, tag="s8", align_bytes=64)
+            live[("x2", q)] = x2
+
+        def op_xt(q, a):
+            x2 = live[("x2", q)]
+            tp = psum.tile([P, 2, 2, 128], F32, tag="tp", bufs=2)
+            for r in range(2):
+                for u in range(2):
+                    nc.tensor.transpose(tp[:, r, u, :], x2[:, 2 * a + r, u, :], ident[:])
+            live[("xp", q, a)] = tp
+
+        def op_ex(q, a):
+            if a == 0:
+                xti_new = shared.tile([P, 4096], BF16, tag="s8", align_bytes=64)
+                live[("xti", q)] = xti_new
+            xti = live[("xti", q)]
             xtw = xti[:].bitcast(F32).rearrange("k (ph a r c u) -> k a ph r c u", ph=2, a=4, r=2, c=64, u=2)
-            for a in range(4):
-                tp = tpool.tile([P, 2, 2, 128], F32, tag="tp")
-                for r in range(2):
-                    for u in range(2):
-                        nc.tensor.transpose(tp[:, r, u, :], x2[:, 2 * a + r, u, :], ident[:])
-                nc.scalar.copy(out=xtw[:, a], in_=tp[:].rearrange("k r u (c ph) -> k ph r c u", ph=2))
+            tp = live[("xp", q, a)]
+            nc.scalar.copy(out=xtw[:, a], in_=tp[:].rearrange("k r u (c ph) -> k ph r c u", ph=2))
+
+        def op_qx(q):
+            xti = live[("xti", q)]
             nc.vector.quantize_mx(out=xt_c[:, q, :].bitcast(E4), scales=xt_s[:, q, :], in_=xti[:])
 
-        def a_prep(g, wr, mr):
+        def op_tt(g):
+            wr, mr = live[("a", g)]
             nc.vector.tensor_tensor(out=mw[:, g, :], in0=wr[:], in1=mr[:], op=ALU.mult)
+
+        def op_aiv(g):
             ai = shared.tile([P, 512, 2, 4], BF16, tag="s8", align_bytes=64)
             nc.vector.tensor_scalar(
                 out=ai[:],
@@ -129,91 +218,92 @@ def tile_gcnfast_t_v_kernel(tc, h, e, AA_mask, GCW, GCB, z, grad_out, out_0, out
                 scalar2=None,
                 op0=ALU.max,
             )
+            live[("ai", g)] = ai
+
+        def op_ais(g):
+            ai = shared.tile([P, 512, 2, 4], BF16, tag="s8", align_bytes=64)
+            nc.scalar.activation(
+                out=ai[:], in_=mw[:, g, :].rearrange("p (j ph x) -> p x ph j", j=4, ph=2), func=ACTF.Relu
+            )
+            live[("ai", g)] = ai
+
+        def op_qaa(g):
+            ai = live[("ai", g)]
             nc.vector.quantize_mx(
                 out=a_c[:, g, :].bitcast(E4),
                 scales=a_s[:, g, :],
                 in_=ai[:].rearrange("p x ph j -> p (x ph j)"),
             )
 
-        def gx(q):
-            for rh in range(2):
-                oh = shared.tile([P, 4, 4, 128], F32, tag="s8", align_bytes=64)
-                for r in range(4):
-                    cols = slice(128 * (4 * rh + r), 128 * (4 * rh + r + 1))
-                    acc = apool.tile([P, 512], F32, tag="acc")
-                    for g in range(2):
-                        nc.tensor.matmul_mx(
-                            out=acc[:],
-                            lhsT=a_c[:, g, cols].bitcast(E4),
-                            lhsT_scale=a_s[:, g, cols],
-                            rhs=da_c[:, q, g, :].bitcast(E5),
-                            rhs_scale=da_s[:, q, g, :],
-                            start=(g == 0),
-                            stop=(g == 1),
-                        )
-                    nc.scalar.copy(out=oh[:, :, r, :], in_=acc[:].rearrange("p (b d) -> p b d", b=4))
+        def op_gx(q, r):
+            cols = slice(128 * r, 128 * (r + 1))
+            acc = psum.tile([P, 512], F32, tag="gx", bufs=2)
+            for g in range(2):
+                nc.tensor.matmul_mx(
+                    out=acc[:],
+                    lhsT=a_c[:, g, cols].bitcast(E4),
+                    lhsT_scale=a_s[:, g, cols],
+                    rhs=da_c[:, q, g, :].bitcast(E5),
+                    rhs_scale=da_s[:, q, g, :],
+                    start=(g == 0),
+                    stop=(g == 1),
+                )
+            live[("gx", q, r)] = acc
+
+        def op_eo(q, r):
+            rh = r // 4
+            if r % 4 == 0:
+                oh_new = shared.tile([P, 4, 4, 128], F32, tag="s8", align_bytes=64)
+                live[("oh", q, rh)] = oh_new
+            oh = live[("oh", q, rh)]
+            acc = live[("gx", q, r)]
+            nc.scalar.copy(out=oh[:, :, r % 4, :], in_=acc[:].rearrange("p (b d) -> p b d", b=4))
+            if r % 4 == 3:
                 nc.scalar.dma_start(
                     out=o0_v[rh][:, 4 * q : 4 * q + 4, :], in_=oh[:].rearrange("p b r d -> p b (r d)")
                 )
 
-        def da(g):
-            for jj in range(4):
-                wo = stream.tile([P, 1024], F32, tag="wo", bufs=3)
-                cols = slice(512 * g + 128 * jj, 512 * g + 128 * (jj + 1))
-                for nh in range(2):
-                    ncols = slice(512 * nh, 512 * (nh + 1))
-                    acc = apool.tile([P, 512], F32, tag="acc")
-                    for q in range(4):
-                        nc.tensor.matmul_mx(
-                            out=acc[:],
-                            lhsT=dt_c[:, q, cols].bitcast(E5),
-                            lhsT_scale=dt_s[:, q, cols],
-                            rhs=xt_c[:, q, ncols].bitcast(E4),
-                            rhs_scale=xt_s[:, q, ncols],
-                            start=(q == 0),
-                            stop=(q == 3),
-                        )
-                    nc.vector.scalar_tensor_tensor(
-                        out=wo[:, ncols],
-                        in0=mw[:, g, 1024 * jj + 512 * nh : 1024 * jj + 512 * (nh + 1)],
-                        scalar=0.0,
-                        in1=acc[:],
-                        op0=ALU.is_gt,
-                        op1=ALU.mult,
-                    )
+        def op_da(g, grp):
+            jj, nh = grp // 2, grp % 2
+            cols = slice(512 * g + 128 * jj, 512 * g + 128 * (jj + 1))
+            ncols = slice(512 * nh, 512 * (nh + 1))
+            acc = psum.tile([P, 512], F32, tag="da", bufs=4)
+            for q in range(4):
+                nc.tensor.matmul_mx(
+                    out=acc[:],
+                    lhsT=dt_c[:, q, cols].bitcast(E5),
+                    lhsT_scale=dt_s[:, q, cols],
+                    rhs=xt_c[:, q, ncols].bitcast(E4),
+                    rhs_scale=xt_s[:, q, ncols],
+                    start=(q == 0),
+                    stop=(q == 3),
+                )
+            live[("da", g, grp)] = acc
+
+        def op_e1(g, grp):
+            jj, nh = grp // 2, grp % 2
+            if nh == 0:
+                wo_new = stream.tile([P, 1024], F32, tag="wo", bufs=3)
+                live[("wo", g, jj)] = wo_new
+            wo = live[("wo", g, jj)]
+            acc = live[("da", g, grp)]
+            nc.vector.scalar_tensor_tensor(
+                out=wo[:, 512 * nh : 512 * (nh + 1)],
+                in0=mw[:, g, 1024 * jj + 512 * nh : 1024 * jj + 512 * (nh + 1)],
+                scalar=0.0,
+                in1=acc[:],
+                op0=ALU.is_gt,
+                op1=ALU.mult,
+            )
+            if nh == 1:
                 nc.sync.dma_start(out=o1_v[g, jj], in_=wo[:])
 
-        u00 = load_unit(0, 0)
-        h0 = load_h(0)
-        u10 = load_unit(1, 0)
-        h1 = load_h(1)
-        unit(0, 0, u00[0], u00[1])
-        xpath(0, h0)
-        u20 = load_unit(2, 0)
-        h2 = load_h(2)
-        unit(1, 0, u10[0], u10[1])
-        xpath(1, h1)
-        u30 = load_unit(3, 0)
-        h3 = load_h(3)
-        unit(2, 0, u20[0], u20[1])
-        xpath(2, h2)
-        a0 = load_a(0)
-        a1 = load_a(1)
-        u01 = load_unit(0, 1)
-        unit(3, 0, u30[0], u30[1])
-        xpath(3, h3)
-        u11 = load_unit(1, 1)
-        a_prep(0, a0[0], a0[1])
-        a_prep(1, a1[0], a1[1])
-        da(0)
-        unit(0, 1, u01[0], u01[1])
-        u21 = load_unit(2, 1)
-        gx(0)
-        unit(1, 1, u11[0], u11[1])
-        u31 = load_unit(3, 1)
-        gx(1)
-        unit(2, 1, u21[0], u21[1])
-        gx(2)
-        unit(3, 1, u31[0], u31[1])
-        gx(3)
-        da(1)
+        ops = {
+            "LU": op_lu, "LH": op_lh, "LA": op_la, "stt": op_stt, "T": op_t, "ed": op_ed,
+            "ilv": op_ilv, "ilvS": op_ilvs, "qa": op_qa, "qb": op_qb, "x2": op_x2, "xT": op_xt,
+            "ex": op_ex, "qx": op_qx, "tt": op_tt, "aiV": op_aiv, "aiS": op_ais, "qA": op_qaa,
+            "gx": op_gx, "eo": op_eo, "da": op_da, "e1": op_e1,
+        }
+        ctx.enter_context(tc.manual_schedule())
+        for op in ORDER:
+            ops[op[0]](*op[1:])

@@ -61,11 +61,11 @@ ORDER = [
 def tile_gcnfast_t_v_kernel(tc, h, e, AA_mask, GCW, GCB, z, grad_out, out_0, out_1):
     nc = tc.nc
 
-    z_v = z.rearrange("b (t g r j) d -> b g t r (j d)", t=16, g=2, r=8, j=4)
-    go_v = grad_out.rearrange("b (g r j) t d -> b g t (r j) d", g=2, r=8, j=4)
-    w_v = GCW.rearrange("(t g r j) w -> g t r (j w)", t=16, g=2, r=8, j=4)
-    m_v = AA_mask.rearrange("(t g r j) w -> g t r (j w)", t=16, g=2, r=8, j=4)
-    o1_v = out_1.rearrange("(t g r j) w -> g j t r w", t=16, g=2, r=8, j=4)
+    z_v = z.rearrange("b (g p j) d -> g p b (j d)", g=2, p=128, j=4)
+    go_v = grad_out.rearrange("b s (g tl) d -> b g tl s d", g=2, tl=8)
+    w_v = GCW.rearrange("(g p j) w -> g p (j w)", g=2, p=128, j=4)
+    m_v = AA_mask.rearrange("(g p j) w -> g p (j w)", g=2, p=128, j=4)
+    o1_v = out_1.rearrange("(g p j) w -> g j p w", g=2, p=128, j=4)
     h_v = h.rearrange("b c (ph r) d -> (c ph) b (r d)", ph=2, r=8)
     o0_v = out_0.rearrange("b c (ph rh r) d -> rh (c ph) b (r d)", ph=2, rh=2, r=4)
 
@@ -94,9 +94,9 @@ def tile_gcnfast_t_v_kernel(tc, h, e, AA_mask, GCW, GCB, z, grad_out, out_0, out
             q, g = n % 4, n // 4
             zu = stream.tile([P, 4, 512], F32, tag="zu", bufs=4)
             gu = stream.tile([P, 4, 512], BF16, tag="gu", bufs=4)
+            nc.sync.dma_start(out=zu[:], in_=z_v[g][:, 4 * q : 4 * q + 4, :])
             for bl in range(4):
                 b = 4 * q + bl
-                nc.sync.dma_start(out=zu[:, bl, :], in_=z_v[b, g])
                 nc.sync.dma_start(out=gu[:, bl, :].rearrange("p (j d) -> p j d", j=4), in_=go_v[b, g])
             live[("u", n)] = (zu, gu)
 

@@ -10,300 +10,325 @@ F32 = mybir.dt.float32
 BF16 = mybir.dt.bfloat16
 U32 = mybir.dt.uint32
 U8 = mybir.dt.uint8
-E4 = mybir.dt.float8_e4m3fn_x4
-E5 = mybir.dt.float8_e5m2_x4
+E4M3 = mybir.dt.float8_e4m3fn_x4
+E5M2 = mybir.dt.float8_e5m2_x4
 ALU = mybir.AluOpType
-ACTF = mybir.ActivationFunctionType
+RELU = mybir.ActivationFunctionType.Relu
 
 P = 128
+PACK = 4
+BANK = 512
 
-ORDER = [
-    ("LU", 0), ("LH", 0), ("stt", 0), ("LA", 1), ("LA", 0), ("T", 0, 0),
-    ("ilv", 0), ("tt", 1), ("qa", 0), ("ed", 0, 0), ("T", 0, 1), ("LU", 1),
-    ("LH", 1), ("tt", 0), ("stt", 1), ("LH", 2), ("x2", 0), ("xT", 0, 0),
-    ("ilv", 1), ("ed", 0, 1), ("xT", 0, 1), ("ex", 0, 0), ("LU", 2), ("ex", 0, 1),
-    ("aiV", 0), ("xT", 0, 2), ("LU", 3), ("ex", 0, 2), ("xT", 0, 3), ("ex", 0, 3),
-    ("aiS", 1), ("T", 1, 0), ("qx", 0), ("ed", 1, 0), ("x2", 1), ("x2", 2),
-    ("xT", 1, 0), ("stt", 2), ("T", 1, 1), ("qb", 0), ("ex", 1, 0), ("qa", 1),
-    ("xT", 1, 1), ("ed", 1, 1), ("qA", 0), ("xT", 2, 0), ("ex", 1, 1), ("ex", 2, 0),
-    ("xT", 1, 2), ("xT", 1, 3), ("ex", 1, 2), ("stt", 3), ("ilv", 2), ("qb", 1),
-    ("qA", 1), ("T", 2, 0), ("ex", 1, 3), ("qa", 2), ("LH", 3), ("T", 2, 1),
-    ("ed", 2, 0), ("ed", 2, 1), ("LU", 4), ("qb", 2), ("xT", 2, 1), ("stt", 4),
-    ("xT", 2, 2), ("x2", 3), ("ex", 2, 1), ("ex", 2, 2), ("xT", 2, 3), ("xT", 3, 0),
-    ("ex", 2, 3), ("ilv", 4), ("LU", 7), ("ex", 3, 0), ("T", 3, 1), ("qa", 4),
-    ("T", 3, 0), ("qx", 1), ("ed", 3, 0), ("gx", 0, 0), ("ilv", 3), ("qx", 2),
-    ("gx", 0, 1), ("ed", 3, 1), ("xT", 3, 1), ("eo", 0, 0), ("eo", 0, 1), ("gx", 0, 2),
-    ("LU", 5), ("LU", 6), ("ex", 3, 1), ("eo", 0, 2), ("xT", 3, 2), ("xT", 3, 3),
-    ("ex", 3, 2), ("gx", 0, 3), ("gx", 0, 4), ("qb", 3), ("ex", 3, 3), ("eo", 0, 3),
-    ("qx", 3), ("da", 0, 0), ("T", 4, 0), ("ed", 4, 0), ("stt", 5), ("ilv", 5),
-    ("gx", 0, 5), ("da", 0, 1), ("qa", 5), ("eo", 0, 4), ("T", 4, 1), ("gx", 0, 6),
-    ("qa", 3), ("eo", 0, 5), ("ed", 4, 1), ("T", 5, 0), ("gx", 1, 0), ("eo", 0, 6),
-    ("stt", 6), ("ed", 5, 0), ("gx", 1, 1), ("da", 0, 2), ("eo", 1, 0), ("e1", 0, 0),
-    ("eo", 1, 1), ("gx", 1, 2), ("gx", 1, 3), ("eo", 1, 2), ("eo", 1, 3), ("e1", 0, 1),
-    ("da", 0, 3), ("gx", 0, 7), ("T", 6, 0), ("eo", 0, 7), ("gx", 1, 4), ("ilv", 6),
-    ("e1", 0, 2), ("qa", 6), ("T", 5, 1), ("eo", 1, 4), ("gx", 1, 5), ("qb", 4),
-    ("gx", 1, 6), ("stt", 7), ("ed", 5, 1), ("eo", 1, 5), ("da", 0, 4), ("e1", 0, 3),
-    ("gx", 1, 7), ("eo", 1, 6), ("ed", 6, 0), ("ilv", 7), ("da", 0, 5), ("eo", 1, 7),
-    ("qa", 7), ("T", 6, 1), ("e1", 0, 4), ("gx", 2, 0), ("e1", 0, 5), ("T", 7, 0),
-    ("eo", 2, 0), ("gx", 2, 1), ("gx", 2, 2), ("eo", 2, 1), ("da", 0, 6), ("eo", 2, 2),
-    ("gx", 3, 0), ("ed", 6, 1), ("eo", 3, 0), ("gx", 2, 3), ("da", 0, 7), ("eo", 2, 3),
-    ("gx", 2, 4), ("qb", 5), ("qb", 6), ("ed", 7, 0), ("gx", 2, 5), ("e1", 0, 6),
-    ("eo", 2, 4), ("gx", 2, 6), ("eo", 2, 5), ("gx", 2, 7), ("eo", 2, 6), ("T", 7, 1),
-    ("eo", 2, 7), ("ed", 7, 1), ("qb", 7), ("gx", 3, 1), ("gx", 3, 2), ("da", 1, 2),
-    ("eo", 3, 1), ("eo", 3, 2), ("gx", 3, 3), ("da", 1, 1), ("eo", 3, 3), ("gx", 3, 4),
-    ("e1", 0, 7), ("da", 1, 0), ("e1", 1, 0), ("gx", 3, 5), ("da", 1, 3), ("eo", 3, 4),
-    ("e1", 1, 1), ("gx", 3, 7), ("eo", 3, 5), ("e1", 1, 2), ("gx", 3, 6), ("da", 1, 6),
-    ("eo", 3, 6), ("da", 1, 4), ("e1", 1, 3), ("da", 1, 7), ("e1", 1, 6), ("da", 1, 5),
-    ("e1", 1, 7), ("e1", 1, 4), ("eo", 3, 7), ("e1", 1, 5),
-]
+UNIT_BUFS = 4
+SHARED_BUFS = 8
+T_BANKS = 2
+SUM_BANKS = 6
+GX_AHEAD = 2
+
+EARLY_GROUPS = (0, 1, 2, 3, 4, 5)
+LATE_GROUPS = (6, 7)
 
 
 def tile_gcnfast_t_v_kernel(tc, h, e, AA_mask, GCW, GCB, z, grad_out, out_0, out_1):
     nc = tc.nc
 
-    z_v = z.rearrange("b (g p j) d -> g p b (j d)", g=2, p=128, j=4)
+    z_v = z.rearrange("b (g p f) d -> g p b (f d)", g=2, p=P, f=PACK)
+    w_v = GCW.rearrange("(g p f) j -> g p (f j)", g=2, p=P, f=PACK)
+    m_v = AA_mask.rearrange("(g p f) j -> g p (f j)", g=2, p=P, f=PACK)
+    o1_v = out_1.rearrange("(g p f) j -> g f p j", g=2, p=P, f=PACK)
     go_v = grad_out.rearrange("b s (g tl) d -> b g tl s d", g=2, tl=8)
-    w_v = GCW.rearrange("(g p j) w -> g p (j w)", g=2, p=128, j=4)
-    m_v = AA_mask.rearrange("(g p j) w -> g p (j w)", g=2, p=128, j=4)
-    o1_v = out_1.rearrange("(g p j) w -> g j p w", g=2, p=128, j=4)
-    h_v = h.rearrange("b c (ph r) d -> (c ph) b (r d)", ph=2, r=8)
-    o0_v = out_0.rearrange("b c (ph rh r) d -> rh (c ph) b (r d)", ph=2, rh=2, r=4)
+    h_v = h.rearrange("b c (th r) d -> (c th) b (r d)", th=2, r=8)
+    o0_v = out_0.rearrange("b c (th rh r) d -> rh (c th) b (r d)", th=2, rh=2, r=4)
 
     with ExitStack() as ctx:
         keep = ctx.enter_context(tc.tile_pool(name="keep", bufs=1))
         stream = ctx.enter_context(tc.tile_pool(name="stream", bufs=2))
-        shared = ctx.enter_context(tc.tile_pool(name="shared", bufs=8))
+        shared = ctx.enter_context(tc.tile_pool(name="shared", bufs=SHARED_BUFS))
         psum = ctx.enter_context(tc.psum_pool(name="psum", bufs=2))
 
         ident = keep.tile([P, P], F32)
         make_identity(nc, ident[:])
 
-        mw = keep.tile([P, 2, 4096], BF16)
-        a_c = keep.tile([P, 2, 1024], U32, align_bytes=64)
-        a_s = keep.tile([P, 2, 1024], U8, align_bytes=64)
-        xt_c = keep.tile([P, 4, 1024], U32, align_bytes=64)
-        xt_s = keep.tile([P, 4, 1024], U8, align_bytes=64)
-        da_c = keep.tile([P, 4, 2, 512], U32, align_bytes=64)
-        da_s = keep.tile([P, 4, 2, 512], U8, align_bytes=64)
-        dt_c = keep.tile([P, 4, 1024], U32, align_bytes=64)
-        dt_s = keep.tile([P, 4, 1024], U8, align_bytes=64)
+        mw = keep.tile([P, 2, PACK * 1024], BF16)
+        a_codes = keep.tile([P, 2, 1024], U32, align_bytes=64)
+        a_scales = keep.tile([P, 2, 1024], U8, align_bytes=64)
+        x_codes = keep.tile([P, 4, 1024], U32, align_bytes=64)
+        x_scales = keep.tile([P, 4, 1024], U8, align_bytes=64)
+        dzi_codes = keep.tile([P, 4, 2, BANK], U32, align_bytes=64)
+        dzi_scales = keep.tile([P, 4, 2, BANK], U8, align_bytes=64)
+        dzk_codes = keep.tile([P, 4, 1024], U32, align_bytes=64)
+        dzk_scales = keep.tile([P, 4, 1024], U8, align_bytes=64)
 
-        live = {}
+        tiles = {}
 
-        def op_lu(n):
-            q, g = n % 4, n // 4
-            zu = stream.tile([P, 4, 512], F32, tag="zu", bufs=4)
-            gu = stream.tile([P, 4, 512], BF16, tag="gu", bufs=4)
-            nc.sync.dma_start(out=zu[:], in_=z_v[g][:, 4 * q : 4 * q + 4, :])
+        def load_unit(n):
+            g, q = n // 4, n % 4
+            z_t = stream.tile([P, 4, PACK * 128], F32, tag="z", bufs=UNIT_BUFS)
+            go_t = stream.tile([P, 4, PACK * 128], BF16, tag="go", bufs=UNIT_BUFS)
+            nc.sync.dma_start(out=z_t[:], in_=z_v[g][:, 4 * q : 4 * q + 4, :])
             for bl in range(4):
-                b = 4 * q + bl
-                nc.sync.dma_start(out=gu[:, bl, :].rearrange("p (j d) -> p j d", j=4), in_=go_v[b, g])
-            live[("u", n)] = (zu, gu)
+                nc.sync.dma_start(
+                    out=go_t[:, bl, :].rearrange("p (f d) -> p f d", f=PACK), in_=go_v[4 * q + bl, g]
+                )
+            tiles[("unit", n)] = (z_t, go_t)
 
-        def op_lh(q):
-            hq = shared.tile([P, 4, 1024], BF16, tag="s8", align_bytes=64)
-            nc.sync.dma_start(out=hq[:], in_=h_v[:, 4 * q : 4 * q + 4, :])
-            live[("h", q)] = hq
+        def load_h(q):
+            h_t = shared.tile([P, 4, 1024], BF16, tag="slot", align_bytes=64)
+            nc.sync.dma_start(out=h_t[:], in_=h_v[:, 4 * q : 4 * q + 4, :])
+            tiles[("h", q)] = h_t
 
-        def op_la(g):
-            wr = shared.tile([P, 4096], BF16, tag="s8", align_bytes=64)
-            mr = shared.tile([P, 4096], BF16, tag="s8", align_bytes=64)
-            nc.sync.dma_start(out=wr[:], in_=w_v[g])
-            nc.sync.dma_start(out=mr[:], in_=m_v[g])
-            live[("a", g)] = (wr, mr)
+        def load_weight(g):
+            w_t = shared.tile([P, PACK * 1024], BF16, tag="slot", align_bytes=64)
+            m_t = shared.tile([P, PACK * 1024], BF16, tag="slot", align_bytes=64)
+            nc.sync.dma_start(out=w_t[:], in_=w_v[g])
+            nc.sync.dma_start(out=m_t[:], in_=m_v[g])
+            tiles[("weight", g)] = (w_t, m_t)
 
-        def op_stt(n):
-            zu, gu = live[("u", n)]
-            du = stream.tile([P, 4, 512], BF16, tag="du", bufs=2, align_bytes=64)
+        def mask_gradient(n):
+            z_t, go_t = tiles[("unit", n)]
+            dz_t = stream.tile([P, PACK, BANK], BF16, tag="dz", align_bytes=64)
             for bl in range(4):
                 nc.vector.scalar_tensor_tensor(
-                    out=du[:, :, 128 * bl : 128 * (bl + 1)],
-                    in0=zu[:, bl, :].rearrange("p (j d) -> p j d", j=4),
+                    out=dz_t[:, :, 128 * bl : 128 * (bl + 1)],
+                    in0=z_t[:, bl, :].rearrange("p (f d) -> p f d", f=PACK),
                     scalar=0.0,
-                    in1=gu[:, bl, :].rearrange("p (j d) -> p j d", j=4),
+                    in1=go_t[:, bl, :].rearrange("p (f d) -> p f d", f=PACK),
                     op0=ALU.is_gt,
                     op1=ALU.mult,
                 )
-            live[("d", n)] = du
+            tiles[("dz", n)] = dz_t
 
-        def op_t(n, a):
-            du = live[("d", n)]
-            dw = du[:].rearrange("p j c -> p (j c)").bitcast(F32)
-            tp = psum.tile([P, 2, 2, 128], F32, tag="tp", bufs=2)
-            for j in range(2):
-                jj = 2 * a + j
-                for u in range(2):
-                    nc.tensor.transpose(tp[:, j, u, :], dw[:, 256 * jj + u : 256 * (jj + 1) : 2], ident[:])
-            live[("tp", n, a)] = tp
+        def transpose_dz(n):
+            words = tiles[("dz", n)][:].rearrange("p f k -> p (f k)").bitcast(F32)
+            for half in range(2):
+                bank = psum.tile([P, 2, 2, P], F32, tag="t", bufs=T_BANKS)
+                for fl in range(2):
+                    first = 256 * (2 * half + fl)
+                    for u in range(2):
+                        nc.tensor.transpose(bank[:, fl, u, :], words[:, first + u : first + 256 : 2], ident[:])
+                tiles[("dz_t", n, half)] = bank
 
-        def op_ed(n, a):
-            if a == 0:
-                dti_new = stream.tile([P, 2048], BF16, tag="dti", bufs=2, align_bytes=64)
-                live[("dti", n)] = dti_new
-            dti = live[("dti", n)]
-            dtw = dti[:].bitcast(F32).rearrange("k (a j p u) -> k a j p u", a=2, j=2, p=128, u=2)
-            tp = live[("tp", n, a)]
-            nc.scalar.copy(out=dtw[:, a], in_=tp[:].rearrange("k j u p -> k j p u"))
+        def copy_dz_t(n):
+            grouped = stream.tile([P, PACK * BANK], BF16, tag="dzk", align_bytes=64)
+            words = grouped[:].bitcast(F32).rearrange("k (half fl i u) -> k half fl i u", half=2, fl=2, i=P, u=2)
+            for half in range(2):
+                bank = tiles[("dz_t", n, half)]
+                nc.scalar.copy(out=words[:, half], in_=bank[:].rearrange("k fl u i -> k fl i u"))
+            tiles[("dzk", n)] = grouped
 
-        def op_ilv(n):
-            du = live[("d", n)]
-            di = stream.tile([P, 512, 4], BF16, tag="di", bufs=2, align_bytes=64)
-            nc.vector.tensor_copy(out=di[:], in_=du[:].rearrange("p j c -> p c j"))
-            live[("di", n)] = di
-
-        def op_ilvs(n):
-            du = live[("d", n)]
-            di = stream.tile([P, 512, 4], BF16, tag="di", bufs=2, align_bytes=64)
-            nc.scalar.copy(out=di[:], in_=du[:].rearrange("p j c -> p c j"))
-            live[("di", n)] = di
-
-        def op_qa(n):
-            q, g = n % 4, n // 4
-            di = live[("di", n)]
+        def quantize_dz_k(n):
+            g, q = n // 4, n % 4
+            cols = slice(BANK * g, BANK * (g + 1))
             nc.vector.quantize_mx(
-                out=da_c[:, q, g, :].bitcast(E5),
-                scales=da_s[:, q, g, :],
-                in_=di[:].rearrange("p c j -> p (c j)"),
+                out=dzk_codes[:, q, cols].bitcast(E5M2), scales=dzk_scales[:, q, cols], in_=tiles[("dzk", n)][:]
             )
 
-        def op_qb(n):
-            q, g = n % 4, n // 4
-            dti = live[("dti", n)]
+        def interleave_dz(n):
+            grouped = stream.tile([P, BANK, PACK], BF16, tag="dzi", align_bytes=64)
+            nc.vector.tensor_copy(out=grouped[:], in_=tiles[("dz", n)][:].rearrange("p f k -> p k f"))
+            tiles[("dzi", n)] = grouped
+
+        def quantize_dz_i(n):
+            g, q = n // 4, n % 4
             nc.vector.quantize_mx(
-                out=dt_c[:, q, 512 * g : 512 * (g + 1)].bitcast(E5),
-                scales=dt_s[:, q, 512 * g : 512 * (g + 1)],
-                in_=dti[:],
+                out=dzi_codes[:, q, g, :].bitcast(E5M2),
+                scales=dzi_scales[:, q, g, :],
+                in_=tiles[("dzi", n)][:].rearrange("p k f -> p (k f)"),
             )
 
-        def op_x2(q):
-            hq = live[("h", q)]
-            hw = hq[:].rearrange("p b x -> p (b x)").bitcast(F32)
-            hw = hw.rearrange("p (b r k u) -> p u r b k", b=4, r=8, k=32, u=2)
-            x2 = shared.tile([P, 8, 2, 128], F32, tag="s8", align_bytes=64)
+        def regroup_x(q):
+            words = tiles[("h", q)][:].rearrange("p b x -> p (b x)").bitcast(F32)
+            words = words.rearrange("p (b r k u) -> p u r b k", b=4, r=8, k=32, u=2)
+            x_t = shared.tile([P, 8, 2, P], F32, tag="slot", align_bytes=64)
             for u in range(2):
-                nc.scalar.copy(out=x2[:, :, u, :].rearrange("p r (b k) -> p r b k", b=4), in_=hw[:, u])
-            live[("x2", q)] = x2
+                nc.scalar.copy(out=x_t[:, :, u, :].rearrange("p r (b k) -> p r b k", b=4), in_=words[:, u])
+            tiles[("x", q)] = x_t
 
-        def op_xt(q, a):
-            x2 = live[("x2", q)]
-            tp = psum.tile([P, 2, 2, 128], F32, tag="tp", bufs=2)
-            for r in range(2):
+        def transpose_x(q, pair):
+            x_t = tiles[("x", q)]
+            bank = psum.tile([P, 2, 2, P], F32, tag="t", bufs=T_BANKS)
+            for rl in range(2):
                 for u in range(2):
-                    nc.tensor.transpose(tp[:, r, u, :], x2[:, 2 * a + r, u, :], ident[:])
-            live[("xp", q, a)] = tp
+                    nc.tensor.transpose(bank[:, rl, u, :], x_t[:, 2 * pair + rl, u, :], ident[:])
+            tiles[("x_t", q, pair)] = bank
 
-        def op_ex(q, a):
-            if a == 0:
-                xti_new = shared.tile([P, 4096], BF16, tag="s8", align_bytes=64)
-                live[("xti", q)] = xti_new
-            xti = live[("xti", q)]
-            xtw = xti[:].bitcast(F32).rearrange("k (ph a r c u) -> k a ph r c u", ph=2, a=4, r=2, c=64, u=2)
-            tp = live[("xp", q, a)]
-            nc.scalar.copy(out=xtw[:, a], in_=tp[:].rearrange("k r u (c ph) -> k ph r c u", ph=2))
+        def copy_x_t(q, pair):
+            if pair == 0:
+                new_tile = shared.tile([P, PACK * 1024], BF16, tag="slot", align_bytes=64)
+                tiles[("xk", q)] = new_tile
+            words = tiles[("xk", q)][:].bitcast(F32)
+            words = words.rearrange("k (th pair rl c u) -> k pair th rl c u", th=2, pair=4, rl=2, c=64, u=2)
+            bank = tiles[("x_t", q, pair)]
+            nc.scalar.copy(out=words[:, pair], in_=bank[:].rearrange("k rl u (c th) -> k th rl c u", th=2))
 
-        def op_qx(q):
-            xti = live[("xti", q)]
-            nc.vector.quantize_mx(out=xt_c[:, q, :].bitcast(E4), scales=xt_s[:, q, :], in_=xti[:])
-
-        def op_tt(g):
-            wr, mr = live[("a", g)]
-            nc.vector.tensor_tensor(out=mw[:, g, :], in0=wr[:], in1=mr[:], op=ALU.mult)
-
-        def op_aiv(g):
-            ai = shared.tile([P, 512, 2, 4], BF16, tag="s8", align_bytes=64)
-            nc.vector.tensor_scalar(
-                out=ai[:],
-                in0=mw[:, g, :].rearrange("p (j ph x) -> p x ph j", j=4, ph=2),
-                scalar1=0.0,
-                scalar2=None,
-                op0=ALU.max,
-            )
-            live[("ai", g)] = ai
-
-        def op_ais(g):
-            ai = shared.tile([P, 512, 2, 4], BF16, tag="s8", align_bytes=64)
-            nc.scalar.activation(
-                out=ai[:], in_=mw[:, g, :].rearrange("p (j ph x) -> p x ph j", j=4, ph=2), func=ACTF.Relu
-            )
-            live[("ai", g)] = ai
-
-        def op_qaa(g):
-            ai = live[("ai", g)]
+        def quantize_x(q):
             nc.vector.quantize_mx(
-                out=a_c[:, g, :].bitcast(E4),
-                scales=a_s[:, g, :],
-                in_=ai[:].rearrange("p x ph j -> p (x ph j)"),
+                out=x_codes[:, q, :].bitcast(E4M3), scales=x_scales[:, q, :], in_=tiles[("xk", q)][:]
             )
 
-        def op_gx(q, r):
-            cols = slice(128 * r, 128 * (r + 1))
-            acc = psum.tile([P, 512], F32, tag="gx", bufs=2)
+        def mask_weight(g):
+            w_t, m_t = tiles[("weight", g)]
+            nc.vector.tensor_tensor(out=mw[:, g, :], in0=w_t[:], in1=m_t[:], op=ALU.mult)
+
+        def interleave_a(g, engine):
+            grouped = shared.tile([P, 512, 2, PACK], BF16, tag="slot", align_bytes=64)
+            source = mw[:, g, :].rearrange("p (f th rc) -> p rc th f", f=PACK, th=2)
+            if engine == "scalar":
+                nc.scalar.activation(out=grouped[:], in_=source, func=RELU)
+            else:
+                nc.vector.tensor_scalar(out=grouped[:], in0=source, scalar1=0.0, scalar2=None, op0=ALU.max)
+            tiles[("a", g)] = grouped
+
+        def quantize_a(g):
+            nc.vector.quantize_mx(
+                out=a_codes[:, g, :].bitcast(E4M3),
+                scales=a_scales[:, g, :],
+                in_=tiles[("a", g)][:].rearrange("p rc th f -> p (rc th f)"),
+            )
+
+        def gx_tile(q, r):
+            cols = slice(P * r, P * (r + 1))
+            acc = psum.tile([P, BANK], F32, tag="sum", bufs=SUM_BANKS)
             for g in range(2):
                 nc.tensor.matmul_mx(
                     out=acc[:],
-                    lhsT=a_c[:, g, cols].bitcast(E4),
-                    lhsT_scale=a_s[:, g, cols],
-                    rhs=da_c[:, q, g, :].bitcast(E5),
-                    rhs_scale=da_s[:, q, g, :],
+                    lhsT=a_codes[:, g, cols].bitcast(E4M3),
+                    lhsT_scale=a_scales[:, g, cols],
+                    rhs=dzi_codes[:, q, g, :].bitcast(E5M2),
+                    rhs_scale=dzi_scales[:, q, g, :],
                     start=(g == 0),
                     stop=(g == 1),
                 )
-            live[("gx", q, r)] = acc
+            tiles[("gx", q, r)] = acc
 
-        def op_eo(q, r):
-            rh = r // 4
-            if r % 4 == 0:
-                oh_new = shared.tile([P, 4, 4, 128], F32, tag="s8", align_bytes=64)
-                live[("oh", q, rh)] = oh_new
-            oh = live[("oh", q, rh)]
-            acc = live[("gx", q, r)]
-            nc.scalar.copy(out=oh[:, :, r % 4, :], in_=acc[:].rearrange("p (b d) -> p b d", b=4))
-            if r % 4 == 3:
+        def store_gx_tile(q, r):
+            rh, rl = r // 4, r % 4
+            if rl == 0:
+                new_tile = shared.tile([P, 4, 4, 128], F32, tag="slot", align_bytes=64)
+                tiles[("o0", q, rh)] = new_tile
+            o0_t = tiles[("o0", q, rh)]
+            nc.scalar.copy(out=o0_t[:, :, rl, :], in_=tiles[("gx", q, r)][:].rearrange("p (b d) -> p b d", b=4))
+            if rl == 3:
                 nc.scalar.dma_start(
-                    out=o0_v[rh][:, 4 * q : 4 * q + 4, :], in_=oh[:].rearrange("p b r d -> p b (r d)")
+                    out=o0_v[rh][:, 4 * q : 4 * q + 4, :], in_=o0_t[:].rearrange("p b r d -> p b (r d)")
                 )
 
-        def op_da(g, grp):
-            jj, nh = grp // 2, grp % 2
-            cols = slice(512 * g + 128 * jj, 512 * g + 128 * (jj + 1))
-            ncols = slice(512 * nh, 512 * (nh + 1))
-            acc = psum.tile([P, 512], F32, tag="da", bufs=4)
-            for q in range(4):
-                nc.tensor.matmul_mx(
-                    out=acc[:],
-                    lhsT=dt_c[:, q, cols].bitcast(E5),
-                    lhsT_scale=dt_s[:, q, cols],
-                    rhs=xt_c[:, q, ncols].bitcast(E4),
-                    rhs_scale=xt_s[:, q, ncols],
-                    start=(q == 0),
-                    stop=(q == 3),
-                )
-            live[("da", g, grp)] = acc
-
-        def op_e1(g, grp):
-            jj, nh = grp // 2, grp % 2
-            if nh == 0:
-                wo_new = stream.tile([P, 1024], F32, tag="wo", bufs=3)
-                live[("wo", g, jj)] = wo_new
-            wo = live[("wo", g, jj)]
-            acc = live[("da", g, grp)]
-            nc.vector.scalar_tensor_tensor(
-                out=wo[:, 512 * nh : 512 * (nh + 1)],
-                in0=mw[:, g, 1024 * jj + 512 * nh : 1024 * jj + 512 * (nh + 1)],
-                scalar=0.0,
-                in1=acc[:],
-                op0=ALU.is_gt,
-                op1=ALU.mult,
+        def da_pass(g, group, q):
+            f, half = group // 2, group % 2
+            rows = slice(BANK * g + P * f, BANK * g + P * (f + 1))
+            cols = slice(BANK * half, BANK * (half + 1))
+            if q == 0:
+                new_tile = psum.tile([P, BANK], F32, tag="sum", bufs=SUM_BANKS)
+                tiles[("da", g, group)] = new_tile
+            nc.tensor.matmul_mx(
+                out=tiles[("da", g, group)][:],
+                lhsT=dzk_codes[:, q, rows].bitcast(E5M2),
+                lhsT_scale=dzk_scales[:, q, rows],
+                rhs=x_codes[:, q, cols].bitcast(E4M3),
+                rhs_scale=x_scales[:, q, cols],
+                start=(q == 0),
+                stop=(q == 3),
             )
-            if nh == 1:
-                nc.sync.dma_start(out=o1_v[g, jj], in_=wo[:])
 
-        ops = {
-            "LU": op_lu, "LH": op_lh, "LA": op_la, "stt": op_stt, "T": op_t, "ed": op_ed,
-            "ilv": op_ilv, "ilvS": op_ilvs, "qa": op_qa, "qb": op_qb, "x2": op_x2, "xT": op_xt,
-            "ex": op_ex, "qx": op_qx, "tt": op_tt, "aiV": op_aiv, "aiS": op_ais, "qA": op_qaa,
-            "gx": op_gx, "eo": op_eo, "da": op_da, "e1": op_e1,
-        }
+        def da_wave(g, wave):
+            for group in wave:
+                for q in range(4):
+                    da_pass(g, group, q)
+
+        def store_da_wave(g, wave):
+            for group in wave:
+                f, half = group // 2, group % 2
+                if half == 0:
+                    new_tile = stream.tile([P, 1024], F32, tag="o1", bufs=3)
+                    tiles[("o1", g, f)] = new_tile
+                o1_t = tiles[("o1", g, f)]
+                first = 1024 * f + BANK * half
+                nc.vector.scalar_tensor_tensor(
+                    out=o1_t[:, BANK * half : BANK * (half + 1)],
+                    in0=mw[:, g, first : first + BANK],
+                    scalar=0.0,
+                    in1=tiles[("da", g, group)][:],
+                    op0=ALU.is_gt,
+                    op1=ALU.mult,
+                )
+                if half == 1:
+                    nc.sync.dma_start(out=o1_v[g, f], in_=o1_t[:])
+
         ctx.enter_context(tc.manual_schedule())
-        for op in ORDER:
-            ops[op[0]](*op[1:])
+
+        load_unit(0)
+        load_h(0)
+        load_weight(0)
+        load_weight(1)
+        load_unit(1)
+        load_h(1)
+        load_unit(2)
+
+        for q in range(4):
+            if q in (1, 2):
+                load_h(q + 1)
+            if q >= 1:
+                load_unit(q + 2)
+            regroup_x(q)
+            transpose_x(q, 0)
+            transpose_x(q, 1)
+            mask_gradient(q)
+            copy_x_t(q, 0)
+            copy_x_t(q, 1)
+            transpose_x(q, 2)
+            transpose_x(q, 3)
+            copy_x_t(q, 2)
+            copy_x_t(q, 3)
+            transpose_dz(q)
+            copy_dz_t(q)
+            interleave_dz(q)
+            quantize_dz_i(q)
+            if q == 0:
+                mask_weight(0)
+                interleave_a(0, "scalar")
+            if q == 1:
+                quantize_a(1)
+                quantize_a(0)
+            quantize_x(q)
+            quantize_dz_k(q)
+            if q == 0:
+                mask_weight(1)
+                interleave_a(1, "vector")
+            for group in EARLY_GROUPS:
+                da_pass(0, group, q)
+
+        load_unit(6)
+        mask_gradient(4)
+        transpose_dz(4)
+        copy_dz_t(4)
+        interleave_dz(4)
+        quantize_dz_i(4)
+        store_da_wave(0, EARLY_GROUPS[:2])
+        da_wave(0, LATE_GROUPS)
+        load_unit(7)
+        for n in range(4, 8):
+            q = n - 4
+            if n < 7:
+                mask_gradient(n + 1)
+            if n == 4:
+                store_da_wave(0, EARLY_GROUPS[2:])
+            for r in range(8):
+                gx_tile(q, r)
+                if r >= GX_AHEAD:
+                    store_gx_tile(q, r - GX_AHEAD)
+                if r == 3:
+                    if n < 7:
+                        transpose_dz(n + 1)
+                    quantize_dz_k(n)
+                    if n == 4:
+                        store_da_wave(0, LATE_GROUPS)
+                if r == 5 and n < 7:
+                    copy_dz_t(n + 1)
+                    interleave_dz(n + 1)
+                    quantize_dz_i(n + 1)
+            for r in range(8 - GX_AHEAD, 8):
+                store_gx_tile(q, r)
+
+        for wave in ((0, 1, 2, 3), (4, 5, 6, 7)):
+            da_wave(1, wave)
+            store_da_wave(1, wave)

from contextlib import ExitStack

import concourse.mybir as mybir
from concourse.masks import make_identity

FLOPS = 2 * 2 * 1024 * 1024 * 2048
BYTES = (4 + 2 + 2 + 8 + 4 + 8 + 4) * 1024 * 1024

F32 = mybir.dt.float32
BF16 = mybir.dt.bfloat16
U32 = mybir.dt.uint32
U8 = mybir.dt.uint8
E4M3 = mybir.dt.float8_e4m3fn_x4
E5M2 = mybir.dt.float8_e5m2_x4
ALU = mybir.AluOpType
RELU = mybir.ActivationFunctionType.Relu

P = 128
PACK = 4
BANK = 512

UNIT_BUFS = 4
SHARED_BUFS = 8
T_BANKS = 2
SUM_BANKS = 6
GX_AHEAD = 2

EARLY_GROUPS = (0, 1, 2, 3, 4, 5)
LATE_GROUPS = (6, 7)


def tile_gcnfast_t_v_kernel(tc, h, e, AA_mask, GCW, GCB, z, grad_out, out_0, out_1):
    nc = tc.nc

    z_v = z.rearrange("b (g p f) d -> g p b (f d)", g=2, p=P, f=PACK)
    w_v = GCW.rearrange("(g p f) j -> g p (f j)", g=2, p=P, f=PACK)
    m_v = AA_mask.rearrange("(g p f) j -> g p (f j)", g=2, p=P, f=PACK)
    o1_v = out_1.rearrange("(g p f) j -> g f p j", g=2, p=P, f=PACK)
    go_v = grad_out.rearrange("b s (g tl) d -> b g tl s d", g=2, tl=8)
    h_v = h.rearrange("b c (th r) d -> (c th) b (r d)", th=2, r=8)
    o0_v = out_0.rearrange("b c (th rh r) d -> rh (c th) b (r d)", th=2, rh=2, r=4)

    with ExitStack() as ctx:
        keep = ctx.enter_context(tc.tile_pool(name="keep", bufs=1))
        stream = ctx.enter_context(tc.tile_pool(name="stream", bufs=2))
        shared = ctx.enter_context(tc.tile_pool(name="shared", bufs=SHARED_BUFS))
        psum = ctx.enter_context(tc.psum_pool(name="psum", bufs=2))

        ident = keep.tile([P, P], F32)
        make_identity(nc, ident[:])

        mw = keep.tile([P, 2, PACK * 1024], BF16)
        a_codes = keep.tile([P, 2, 1024], U32, align_bytes=64)
        a_scales = keep.tile([P, 2, 1024], U8, align_bytes=64)
        x_codes = keep.tile([P, 4, 1024], U32, align_bytes=64)
        x_scales = keep.tile([P, 4, 1024], U8, align_bytes=64)
        dzi_codes = keep.tile([P, 4, 2, BANK], U32, align_bytes=64)
        dzi_scales = keep.tile([P, 4, 2, BANK], U8, align_bytes=64)
        dzk_codes = keep.tile([P, 4, 1024], U32, align_bytes=64)
        dzk_scales = keep.tile([P, 4, 1024], U8, align_bytes=64)

        tiles = {}

        def load_unit(n):
            g, q = n // 4, n % 4
            z_t = stream.tile([P, 4, PACK * 128], F32, tag="z", bufs=UNIT_BUFS)
            go_t = stream.tile([P, 4, PACK * 128], BF16, tag="go", bufs=UNIT_BUFS)
            nc.sync.dma_start(out=z_t[:], in_=z_v[g][:, 4 * q : 4 * q + 4, :])
            for bl in range(4):
                nc.sync.dma_start(
                    out=go_t[:, bl, :].rearrange("p (f d) -> p f d", f=PACK), in_=go_v[4 * q + bl, g]
                )
            tiles[("unit", n)] = (z_t, go_t)

        def load_h(q):
            h_t = shared.tile([P, 4, 1024], BF16, tag="slot", align_bytes=64)
            nc.sync.dma_start(out=h_t[:], in_=h_v[:, 4 * q : 4 * q + 4, :])
            tiles[("h", q)] = h_t

        def load_weight(g):
            w_t = shared.tile([P, PACK * 1024], BF16, tag="slot", align_bytes=64)
            m_t = shared.tile([P, PACK * 1024], BF16, tag="slot", align_bytes=64)
            nc.sync.dma_start(out=w_t[:], in_=w_v[g])
            nc.sync.dma_start(out=m_t[:], in_=m_v[g])
            tiles[("weight", g)] = (w_t, m_t)

        def mask_gradient(n):
            z_t, go_t = tiles[("unit", n)]
            dz_t = stream.tile([P, PACK, BANK], BF16, tag="dz", align_bytes=64)
            for bl in range(4):
                nc.vector.scalar_tensor_tensor(
                    out=dz_t[:, :, 128 * bl : 128 * (bl + 1)],
                    in0=z_t[:, bl, :].rearrange("p (f d) -> p f d", f=PACK),
                    scalar=0.0,
                    in1=go_t[:, bl, :].rearrange("p (f d) -> p f d", f=PACK),
                    op0=ALU.is_gt,
                    op1=ALU.mult,
                )
            tiles[("dz", n)] = dz_t

        def transpose_dz(n):
            words = tiles[("dz", n)][:].rearrange("p f k -> p (f k)").bitcast(F32)
            for half in range(2):
                bank = psum.tile([P, 2, 2, P], F32, tag="t", bufs=T_BANKS)
                for fl in range(2):
                    first = 256 * (2 * half + fl)
                    for u in range(2):
                        nc.tensor.transpose(bank[:, fl, u, :], words[:, first + u : first + 256 : 2], ident[:])
                tiles[("dz_t", n, half)] = bank

        def copy_dz_t(n):
            grouped = stream.tile([P, PACK * BANK], BF16, tag="dzk", align_bytes=64)
            words = grouped[:].bitcast(F32).rearrange("k (half fl i u) -> k half fl i u", half=2, fl=2, i=P, u=2)
            for half in range(2):
                bank = tiles[("dz_t", n, half)]
                nc.scalar.copy(out=words[:, half], in_=bank[:].rearrange("k fl u i -> k fl i u"))
            tiles[("dzk", n)] = grouped

        def quantize_dz_k(n):
            g, q = n // 4, n % 4
            cols = slice(BANK * g, BANK * (g + 1))
            nc.vector.quantize_mx(
                out=dzk_codes[:, q, cols].bitcast(E5M2), scales=dzk_scales[:, q, cols], in_=tiles[("dzk", n)][:]
            )

        def interleave_dz(n):
            grouped = stream.tile([P, BANK, PACK], BF16, tag="dzi", align_bytes=64)
            nc.vector.tensor_copy(out=grouped[:], in_=tiles[("dz", n)][:].rearrange("p f k -> p k f"))
            tiles[("dzi", n)] = grouped

        def quantize_dz_i(n):
            g, q = n // 4, n % 4
            nc.vector.quantize_mx(
                out=dzi_codes[:, q, g, :].bitcast(E5M2),
                scales=dzi_scales[:, q, g, :],
                in_=tiles[("dzi", n)][:].rearrange("p k f -> p (k f)"),
            )

        def regroup_x(q):
            words = tiles[("h", q)][:].rearrange("p b x -> p (b x)").bitcast(F32)
            words = words.rearrange("p (b r k u) -> p u r b k", b=4, r=8, k=32, u=2)
            x_t = shared.tile([P, 8, 2, P], F32, tag="slot", align_bytes=64)
            for u in range(2):
                nc.scalar.copy(out=x_t[:, :, u, :].rearrange("p r (b k) -> p r b k", b=4), in_=words[:, u])
            tiles[("x", q)] = x_t

        def transpose_x(q, pair):
            x_t = tiles[("x", q)]
            bank = psum.tile([P, 2, 2, P], F32, tag="t", bufs=T_BANKS)
            for rl in range(2):
                for u in range(2):
                    nc.tensor.transpose(bank[:, rl, u, :], x_t[:, 2 * pair + rl, u, :], ident[:])
            tiles[("x_t", q, pair)] = bank

        def copy_x_t(q, pair):
            if pair == 0:
                new_tile = shared.tile([P, PACK * 1024], BF16, tag="slot", align_bytes=64)
                tiles[("xk", q)] = new_tile
            words = tiles[("xk", q)][:].bitcast(F32)
            words = words.rearrange("k (th pair rl c u) -> k pair th rl c u", th=2, pair=4, rl=2, c=64, u=2)
            bank = tiles[("x_t", q, pair)]
            nc.scalar.copy(out=words[:, pair], in_=bank[:].rearrange("k rl u (c th) -> k th rl c u", th=2))

        def quantize_x(q):
            nc.vector.quantize_mx(
                out=x_codes[:, q, :].bitcast(E4M3), scales=x_scales[:, q, :], in_=tiles[("xk", q)][:]
            )

        def mask_weight(g):
            w_t, m_t = tiles[("weight", g)]
            nc.vector.tensor_tensor(out=mw[:, g, :], in0=w_t[:], in1=m_t[:], op=ALU.mult)

        def interleave_a(g, engine):
            grouped = shared.tile([P, 512, 2, PACK], BF16, tag="slot", align_bytes=64)
            source = mw[:, g, :].rearrange("p (f th rc) -> p rc th f", f=PACK, th=2)
            if engine == "scalar":
                nc.scalar.activation(out=grouped[:], in_=source, func=RELU)
            else:
                nc.vector.tensor_scalar(out=grouped[:], in0=source, scalar1=0.0, scalar2=None, op0=ALU.max)
            tiles[("a", g)] = grouped

        def quantize_a(g):
            nc.vector.quantize_mx(
                out=a_codes[:, g, :].bitcast(E4M3),
                scales=a_scales[:, g, :],
                in_=tiles[("a", g)][:].rearrange("p rc th f -> p (rc th f)"),
            )

        def gx_tile(q, r):
            cols = slice(P * r, P * (r + 1))
            acc = psum.tile([P, BANK], F32, tag="sum", bufs=SUM_BANKS)
            for g in range(2):
                nc.tensor.matmul_mx(
                    out=acc[:],
                    lhsT=a_codes[:, g, cols].bitcast(E4M3),
                    lhsT_scale=a_scales[:, g, cols],
                    rhs=dzi_codes[:, q, g, :].bitcast(E5M2),
                    rhs_scale=dzi_scales[:, q, g, :],
                    start=(g == 0),
                    stop=(g == 1),
                )
            tiles[("gx", q, r)] = acc

        def store_gx_tile(q, r):
            rh, rl = r // 4, r % 4
            if rl == 0:
                new_tile = shared.tile([P, 4, 4, 128], F32, tag="slot", align_bytes=64)
                tiles[("o0", q, rh)] = new_tile
            o0_t = tiles[("o0", q, rh)]
            nc.scalar.copy(out=o0_t[:, :, rl, :], in_=tiles[("gx", q, r)][:].rearrange("p (b d) -> p b d", b=4))
            if rl == 3:
                nc.scalar.dma_start(
                    out=o0_v[rh][:, 4 * q : 4 * q + 4, :], in_=o0_t[:].rearrange("p b r d -> p b (r d)")
                )

        def da_pass(g, group, q):
            f, half = group // 2, group % 2
            rows = slice(BANK * g + P * f, BANK * g + P * (f + 1))
            cols = slice(BANK * half, BANK * (half + 1))
            if q == 0:
                new_tile = psum.tile([P, BANK], F32, tag="sum", bufs=SUM_BANKS)
                tiles[("da", g, group)] = new_tile
            nc.tensor.matmul_mx(
                out=tiles[("da", g, group)][:],
                lhsT=dzk_codes[:, q, rows].bitcast(E5M2),
                lhsT_scale=dzk_scales[:, q, rows],
                rhs=x_codes[:, q, cols].bitcast(E4M3),
                rhs_scale=x_scales[:, q, cols],
                start=(q == 0),
                stop=(q == 3),
            )

        def da_wave(g, wave):
            for group in wave:
                for q in range(4):
                    da_pass(g, group, q)

        def store_da_wave(g, wave):
            for group in wave:
                f, half = group // 2, group % 2
                if half == 0:
                    new_tile = stream.tile([P, 1024], F32, tag="o1", bufs=3)
                    tiles[("o1", g, f)] = new_tile
                o1_t = tiles[("o1", g, f)]
                first = 1024 * f + BANK * half
                nc.vector.scalar_tensor_tensor(
                    out=o1_t[:, BANK * half : BANK * (half + 1)],
                    in0=mw[:, g, first : first + BANK],
                    scalar=0.0,
                    in1=tiles[("da", g, group)][:],
                    op0=ALU.is_gt,
                    op1=ALU.mult,
                )
                if half == 1:
                    nc.sync.dma_start(out=o1_v[g, f], in_=o1_t[:])

        ctx.enter_context(tc.manual_schedule())

        load_unit(0)
        load_h(0)
        load_weight(0)
        load_weight(1)
        load_unit(1)
        load_h(1)
        load_unit(2)

        for q in range(4):
            if q in (1, 2):
                load_h(q + 1)
            if q >= 1:
                load_unit(q + 2)
            regroup_x(q)
            transpose_x(q, 0)
            transpose_x(q, 1)
            mask_gradient(q)
            copy_x_t(q, 0)
            copy_x_t(q, 1)
            transpose_x(q, 2)
            transpose_x(q, 3)
            copy_x_t(q, 2)
            copy_x_t(q, 3)
            transpose_dz(q)
            copy_dz_t(q)
            interleave_dz(q)
            quantize_dz_i(q)
            if q == 0:
                mask_weight(0)
                interleave_a(0, "scalar")
            if q == 1:
                quantize_a(1)
                quantize_a(0)
            quantize_x(q)
            quantize_dz_k(q)
            if q == 0:
                mask_weight(1)
                interleave_a(1, "vector")
            for group in EARLY_GROUPS:
                da_pass(0, group, q)

        load_unit(6)
        mask_gradient(4)
        transpose_dz(4)
        copy_dz_t(4)
        interleave_dz(4)
        quantize_dz_i(4)
        store_da_wave(0, EARLY_GROUPS[:2])
        da_wave(0, LATE_GROUPS)
        load_unit(7)
        for n in range(4, 8):
            q = n - 4
            if n < 7:
                mask_gradient(n + 1)
            if n == 4:
                store_da_wave(0, EARLY_GROUPS[2:])
            for r in range(8):
                gx_tile(q, r)
                if r >= GX_AHEAD:
                    store_gx_tile(q, r - GX_AHEAD)
                if r == 3:
                    if n < 7:
                        transpose_dz(n + 1)
                    quantize_dz_k(n)
                    if n == 4:
                        store_da_wave(0, LATE_GROUPS)
                if r == 5 and n < 7:
                    copy_dz_t(n + 1)
                    interleave_dz(n + 1)
                    quantize_dz_i(n + 1)
            for r in range(8 - GX_AHEAD, 8):
                store_gx_tile(q, r)

        for wave in ((0, 1, 2, 3), (4, 5, 6, 7)):
            da_wave(1, wave)
            store_da_wave(1, wave)
